import numpy as np
import ml_dtypes

BF16 = ml_dtypes.bfloat16


def bf(x):
    return np.asarray(x, np.float32).astype(BF16)


def f32(x):
    return np.asarray(x, np.float32)


def f64(x):
    return np.asarray(x).astype(np.float64)


def striped(idx):
    return np.tile(idx.reshape(-1, 16).T, (8, 1))


S, P, D, M, R, N = 256, 128, 16, 256, 4, 1024


def setup_inputs():
    m = np.arange(M)
    p = np.arange(P)
    return {"table": bf(np.random.standard_normal((P, S))), "x_dst": bf(np.random.standard_normal((P, N))), "w_src": bf(np.random.standard_normal((P, M)) / np.sqrt(P + P)), "w_dst": bf(np.random.standard_normal((P, M)) / np.sqrt(P + P)), "grp": bf(p[:, None] // D == p[None, :] // D), "diag": f32((m // D == m % D)[:, None]), "offs": striped(np.concatenate([np.random.permutation(S) for _ in range(R)]))}


def reference(table, x_dst, w_src, w_dst, grp, diag, offs):
    idx = offs[:16].T.reshape(-1)
    maps = f64(w_src).T @ f64(table)[:, idx] + f64(w_dst).T @ f64(x_dst)
    e = np.exp(maps)
    den = np.concatenate([f64(grp).T @ e[h * P:(h + 1) * P] for h in range(M // P)], axis=0)
    return f64(diag) - e / den

@@ -1,0 +1,73 @@
+import concourse.mybir as mybir
+
+BF16, F32, U16 = mybir.dt.bfloat16, mybir.dt.float32, mybir.dt.uint16
+EXP, LN = mybir.ActivationFunctionType.Exp, mybir.ActivationFunctionType.Ln
+MULT, ADD, SUBTRACT = mybir.AluOpType.mult, mybir.AluOpType.add, mybir.AluOpType.subtract
+
+P = 128
+S = 256
+N = 1024
+M = 256
+HALVES = M // P
+BANK = 512
+PIECE = 128
+PIECES = BANK // PIECE
+
+FLOPS = 2 * (2 * P) * M * N + 2 * P * M * N
+
+
+def tile_attentionsheaflearner_kernel(tc, table, x_dst, w_src, w_dst, grp, diag, offs, out):
+    nc = tc.nc
+    units = [(c, h) for c in range(N // BANK) for h in range(HALVES)]
+    with (
+        tc.tile_pool(name="held", bufs=1) as held,
+        tc.tile_pool(name="work", bufs=len(units)) as work,
+        tc.psum_pool(name="maps_pool", bufs=1) as maps_pool,
+        tc.psum_pool(name="den_pool", bufs=len(units)) as den_pool,
+    ):
+        offsets = held.tile([P, N // 16], U16, name="offsets")
+        nc.sync.dma_start(offsets[:], offs)
+        table_sb = held.tile([P, S], BF16, name="table_sb")
+        nc.sync.dma_start(table_sb[:], table)
+        w_src_sb = held.tile([P, M], BF16, name="w_src_sb")
+        nc.scalar.dma_start(w_src_sb[:], w_src)
+        w_dst_sb = held.tile([P, M], BF16, name="w_dst_sb")
+        nc.scalar.dma_start(w_dst_sb[:], w_dst)
+        x_dst_sb = held.tile([P, N], BF16, name="x_dst_sb")
+        nc.sync.dma_start(x_dst_sb[:], x_dst)
+        grp_sb = held.tile([P, P], BF16, name="grp_sb")
+        nc.scalar.dma_start(grp_sb[:], grp)
+        diag_sb = [held.tile([P, 1], F32, name=f"diag_sb{h}") for h in range(HALVES)]
+        for h in range(HALVES):
+            nc.scalar.dma_start(diag_sb[h][:], diag[h * P : (h + 1) * P, :])
+
+        maps = [maps_pool.tile([P, BANK], F32, name=f"maps{u}") for u in range(len(units))]
+        for u, (c, h) in enumerate(units):
+            for k in range(PIECES):
+                piece = c * PIECES + k
+                looked_up = table_sb[:].indirect(offsets[:, piece * (PIECE // 16) : (piece + 1) * (PIECE // 16)])
+                nc.tensor.matmul(
+                    maps[u][:, k * PIECE : (k + 1) * PIECE],
+                    w_src_sb[:, h * P : (h + 1) * P],
+                    looked_up,
+                    start=(k == 0),
+                    stop=False,
+                )
+
+        for u, (c, h) in enumerate(units):
+            half = slice(h * P, (h + 1) * P)
+            cols = slice(c * BANK, (c + 1) * BANK)
+            nc.tensor.matmul(maps[u][:], w_dst_sb[:, half], x_dst_sb[:, cols], start=False, stop=True)
+            e_bf = work.tile([P, BANK], BF16, name="e_bf")
+            nc.scalar.activation(e_bf[:], maps[u][:], EXP)
+            den = den_pool.tile([P, BANK], F32, name="den")
+            nc.tensor.matmul(den[:], grp_sb[:], e_bf[:], start=True, stop=True)
+            ln_den = work.tile([P, BANK], F32, name="ln_den")
+            nc.scalar.activation(ln_den[:], den[:], LN)
+            logit = work.tile([P, BANK], F32, name="logit")
+            nc.vector.tensor_tensor(logit[:], maps[u][:], ln_den[:], SUBTRACT)
+            share = work.tile([P, BANK], F32, name="share")
+            nc.scalar.activation(share[:], logit[:], EXP)
+            res = work.tile([P, BANK], F32, name="res")
+            nc.vector.tensor_scalar(res[:], share[:], -1.0, diag_sb[h][:], MULT, ADD)
+            nc.sync.dma_start(out[half, cols], res[:])

@@ -60,14 +60,14 @@ def tile_attentionsheaflearner_kernel(tc, table, x_dst, w_src, w_dst, grp, diag,
             nc.tensor.matmul(maps[u][:], w_dst_sb[:, half], x_dst_sb[:, cols], start=False, stop=True)
             e_bf = work.tile([P, BANK], BF16, name="e_bf")
             nc.scalar.activation(e_bf[:], maps[u][:], EXP)
+            e = work.tile([P, BANK], F32, name="e")
+            nc.scalar.activation(e[:], maps[u][:], EXP)
             den = den_pool.tile([P, BANK], F32, name="den")
             nc.tensor.matmul(den[:], grp_sb[:], e_bf[:], start=True, stop=True)
-            ln_den = work.tile([P, BANK], F32, name="ln_den")
-            nc.scalar.activation(ln_den[:], den[:], LN)
-            logit = work.tile([P, BANK], F32, name="logit")
-            nc.vector.tensor_tensor(logit[:], maps[u][:], ln_den[:], SUBTRACT)
+            rden = work.tile([P, BANK], F32, name="rden")
+            nc.vector.reciprocal(rden[:], den[:])
             share = work.tile([P, BANK], F32, name="share")
-            nc.scalar.activation(share[:], logit[:], EXP)
+            nc.gpsimd.tensor_tensor(share[:], e[:], rden[:], MULT)
             res = work.tile([P, BANK], F32, name="res")
-            nc.vector.tensor_scalar(res[:], share[:], -1.0, diag_sb[h][:], MULT, ADD)
+            nc.gpsimd.tensor_scalar(res[:], share[:], -1.0, diag_sb[h][:], MULT, ADD)
             nc.sync.dma_start(out[half, cols], res[:])

@@ -23,7 +23,7 @@ def tile_attentionsheaflearner_kernel(tc, table, x_dst, w_src, w_dst, grp, diag,
         tc.tile_pool(name="held", bufs=1) as held,
         tc.tile_pool(name="work", bufs=len(units)) as work,
         tc.psum_pool(name="maps_pool", bufs=1) as maps_pool,
-        tc.psum_pool(name="den_pool", bufs=len(units)) as den_pool,
+        tc.psum_pool(name="den_pool", bufs=1) as den_pool,
     ):
         offsets = held.tile([P, N // 16], U16, name="offsets")
         nc.sync.dma_start(offsets[:], offs)
@@ -54,20 +54,28 @@ def tile_attentionsheaflearner_kernel(tc, table, x_dst, w_src, w_dst, grp, diag,
                     stop=False,
                 )
 
+        den = [den_pool.tile([P, BANK], F32, name=f"den{u}") for u in range(len(units))]
         for u, (c, h) in enumerate(units):
-            half = slice(h * P, (h + 1) * P)
-            cols = slice(c * BANK, (c + 1) * BANK)
-            nc.tensor.matmul(maps[u][:], w_dst_sb[:, half], x_dst_sb[:, cols], start=False, stop=True)
+            nc.tensor.matmul(
+                maps[u][:],
+                w_dst_sb[:, h * P : (h + 1) * P],
+                x_dst_sb[:, c * BANK : (c + 1) * BANK],
+                start=False,
+                stop=True,
+            )
             e_bf = work.tile([P, BANK], BF16, name="e_bf")
             nc.scalar.activation(e_bf[:], maps[u][:], EXP)
-            e = work.tile([P, BANK], F32, name="e")
-            nc.scalar.activation(e[:], maps[u][:], EXP)
-            den = den_pool.tile([P, BANK], F32, name="den")
-            nc.tensor.matmul(den[:], grp_sb[:], e_bf[:], start=True, stop=True)
-            rden = work.tile([P, BANK], F32, name="rden")
-            nc.vector.reciprocal(rden[:], den[:])
+            nc.tensor.matmul(den[u][:], grp_sb[:], e_bf[:], start=True, stop=True)
+
+        logit = [work.tile([P, BANK], F32, name="logit") for u in range(len(units))]
+        for u in range(len(units)):
+            ln_den = work.tile([P, BANK], F32, name="ln_den")
+            nc.scalar.activation(ln_den[:], den[u][:], LN)
+            nc.vector.tensor_tensor(logit[u][:], maps[u][:], ln_den[:], SUBTRACT)
+
+        for u, (c, h) in enumerate(units):
             share = work.tile([P, BANK], F32, name="share")
-            nc.gpsimd.tensor_tensor(share[:], e[:], rden[:], MULT)
+            nc.scalar.activation(share[:], logit[u][:], EXP)
             res = work.tile([P, BANK], F32, name="res")
-            nc.gpsimd.tensor_scalar(res[:], share[:], -1.0, diag_sb[h][:], MULT, ADD)
-            nc.sync.dma_start(out[half, cols], res[:])
+            nc.vector.tensor_scalar(res[:], share[:], -1.0, diag_sb[h][:], MULT, ADD)
+            nc.sync.dma_start(out[h * P : (h + 1) * P, c * BANK : (c + 1) * BANK], res[:])

@@ -1,29 +1,29 @@
 import concourse.mybir as mybir
 
 BF16, F32, U16 = mybir.dt.bfloat16, mybir.dt.float32, mybir.dt.uint16
-EXP, LN = mybir.ActivationFunctionType.Exp, mybir.ActivationFunctionType.Ln
-MULT, ADD, SUBTRACT = mybir.AluOpType.mult, mybir.AluOpType.add, mybir.AluOpType.subtract
+EXP, IDENTITY = mybir.ActivationFunctionType.Exp, mybir.ActivationFunctionType.Identity
+MULT = mybir.AluOpType.mult
 
 P = 128
 S = 256
 N = 1024
 M = 256
-HALVES = M // P
+SIDES = M // P
 BANK = 512
 PIECE = 128
 PIECES = BANK // PIECE
+CHUNK = 256
+CHUNKS = BANK // CHUNK
 
 FLOPS = 2 * (2 * P) * M * N + 2 * P * M * N
 
 
 def tile_attentionsheaflearner_kernel(tc, table, x_dst, w_src, w_dst, grp, diag, offs, out):
     nc = tc.nc
-    units = [(c, h) for c in range(N // BANK) for h in range(HALVES)]
     with (
         tc.tile_pool(name="held", bufs=1) as held,
-        tc.tile_pool(name="work", bufs=len(units)) as work,
-        tc.psum_pool(name="maps_pool", bufs=1) as maps_pool,
-        tc.psum_pool(name="den_pool", bufs=1) as den_pool,
+        tc.tile_pool(name="work", bufs=N // CHUNK) as work,
+        tc.psum_pool(name="psum", bufs=1) as psum,
     ):
         offsets = held.tile([P, N // 16], U16, name="offsets")
         nc.sync.dma_start(offsets[:], offs)
@@ -35,47 +35,61 @@ def tile_attentionsheaflearner_kernel(tc, table, x_dst, w_src, w_dst, grp, diag,
         nc.scalar.dma_start(w_dst_sb[:], w_dst)
         x_dst_sb = held.tile([P, N], BF16, name="x_dst_sb")
         nc.sync.dma_start(x_dst_sb[:], x_dst)
-        grp_sb = held.tile([P, P], BF16, name="grp_sb")
-        nc.scalar.dma_start(grp_sb[:], grp)
-        diag_sb = [held.tile([P, 1], F32, name=f"diag_sb{h}") for h in range(HALVES)]
-        for h in range(HALVES):
-            nc.scalar.dma_start(diag_sb[h][:], diag[h * P : (h + 1) * P, :])
 
-        maps = [maps_pool.tile([P, BANK], F32, name=f"maps{u}") for u in range(len(units))]
-        for u, (c, h) in enumerate(units):
-            for k in range(PIECES):
-                piece = c * PIECES + k
-                looked_up = table_sb[:].indirect(offsets[:, piece * (PIECE // 16) : (piece + 1) * (PIECE // 16)])
+        w_src_side = held.tile([P, SIDES, P], BF16, name="w_src_side")
+        nc.vector.tensor_copy(w_src_side[:], w_src_sb[:].rearrange("d (p side) -> d side p", side=SIDES))
+        w_dst_side = held.tile([P, SIDES, P], BF16, name="w_dst_side")
+        nc.vector.tensor_copy(w_dst_side[:], w_dst_sb[:].rearrange("d (p side) -> d side p", side=SIDES))
+        out_side = out.rearrange("(p side) j -> side p j", side=SIDES)
+        diag_side = diag.rearrange("(p side) one -> side p one", side=SIDES)
+        diag_sb = [held.tile([P, 1], F32, name=f"diag_sb{side}") for side in range(SIDES)]
+        for side in range(SIDES):
+            nc.scalar.dma_start(diag_sb[side][:], diag_side[side])
+
+        grp_rows = held.tile([P, P], BF16, name="grp_rows")
+        grp_side = held.tile([P, P], BF16, name="grp_side")
+        nc.vector.memset(grp_side[:], 0.0)
+        for half in range(2):
+            rows = slice(half * (P // 2), (half + 1) * (P // 2))
+            nc.scalar.dma_start(grp_rows[rows, :], grp.rearrange("(q two) r -> two q r", two=2)[0])
+            nc.vector.tensor_copy(grp_side[rows, rows], grp_rows[:].rearrange("q (r two) -> q two r", two=2)[rows, 0, :])
+
+        banks = range(N // BANK)
+        maps = [[psum.tile([P, BANK], F32, name=f"maps{b}{side}") for side in range(SIDES)] for b in banks]
+        for b in banks:
+            for side in range(SIDES):
+                for k in range(PIECES):
+                    piece = b * PIECES + k
+                    looked_up = table_sb[:].indirect(offsets[:, piece * (PIECE // 16) : (piece + 1) * (PIECE // 16)])
+                    nc.tensor.matmul(
+                        maps[b][side][:, k * PIECE : (k + 1) * PIECE],
+                        w_src_side[:, side, :],
+                        looked_up,
+                        start=(k == 0),
+                        stop=False,
+                    )
+
+        den = [psum.tile([P, CHUNK], F32, name=f"den{c}") for c in range(N // CHUNK)]
+        for b in banks:
+            for side in range(SIDES):
                 nc.tensor.matmul(
-                    maps[u][:, k * PIECE : (k + 1) * PIECE],
-                    w_src_sb[:, h * P : (h + 1) * P],
-                    looked_up,
-                    start=(k == 0),
-                    stop=False,
+                    maps[b][side][:], w_dst_side[:, side, :], x_dst_sb[:, b * BANK : (b + 1) * BANK], start=False, stop=True
                 )
+            for c in range(b * CHUNKS, (b + 1) * CHUNKS):
+                for side in range(SIDES):
+                    e_bf = work.tile([P, CHUNK], BF16, name=f"e_bf{side}")
+                    nc.scalar.activation(e_bf[:], maps[b][side][:, (c - b * CHUNKS) * CHUNK : (c - b * CHUNKS + 1) * CHUNK], EXP)
+                    nc.tensor.matmul(den[c][:], grp_side[:], e_bf[:], start=(side == 0), stop=(side == SIDES - 1))
 
-        den = [den_pool.tile([P, BANK], F32, name=f"den{u}") for u in range(len(units))]
-        for u, (c, h) in enumerate(units):
-            nc.tensor.matmul(
-                maps[u][:],
-                w_dst_sb[:, h * P : (h + 1) * P],
-                x_dst_sb[:, c * BANK : (c + 1) * BANK],
-                start=False,
-                stop=True,
-            )
-            e_bf = work.tile([P, BANK], BF16, name="e_bf")
-            nc.scalar.activation(e_bf[:], maps[u][:], EXP)
-            nc.tensor.matmul(den[u][:], grp_sb[:], e_bf[:], start=True, stop=True)
-
-        logit = [work.tile([P, BANK], F32, name="logit") for u in range(len(units))]
-        for u in range(len(units)):
-            ln_den = work.tile([P, BANK], F32, name="ln_den")
-            nc.scalar.activation(ln_den[:], den[u][:], LN)
-            nc.vector.tensor_tensor(logit[u][:], maps[u][:], ln_den[:], SUBTRACT)
-
-        for u, (c, h) in enumerate(units):
-            share = work.tile([P, BANK], F32, name="share")
-            nc.scalar.activation(share[:], logit[u][:], EXP)
-            res = work.tile([P, BANK], F32, name="res")
-            nc.vector.tensor_scalar(res[:], share[:], -1.0, diag_sb[h][:], MULT, ADD)
-            nc.sync.dma_start(out[h * P : (h + 1) * P, c * BANK : (c + 1) * BANK], res[:])
+        for c in range(N // CHUNK):
+            b = c // CHUNKS
+            rden = work.tile([P, CHUNK], F32, name="rden")
+            nc.vector.reciprocal(rden[:], den[c][:])
+            for side in range(SIDES):
+                e = work.tile([P, CHUNK], F32, name=f"e{side}")
+                nc.scalar.activation(e[:], maps[b][side][:, (c - b * CHUNKS) * CHUNK : (c - b * CHUNKS + 1) * CHUNK], EXP)
+                share = work.tile([P, CHUNK], F32, name=f"share{side}")
+                nc.gpsimd.tensor_tensor(share[:], e[:], rden[:], MULT)
+                res = work.tile([P, CHUNK], F32, name=f"res{side}")
+                nc.scalar.activation(res[:], share[:], IDENTITY, bias=diag_sb[side][:], scale=-1.0)
+                nc.sync.dma_start(out_side[side, :, c * CHUNK : (c + 1) * CHUNK], res[:])

@@ -1,8 +1,9 @@
 import concourse.mybir as mybir
+from concourse.masks import make_identity
 
 BF16, F32, U16 = mybir.dt.bfloat16, mybir.dt.float32, mybir.dt.uint16
 EXP, IDENTITY = mybir.ActivationFunctionType.Exp, mybir.ActivationFunctionType.Identity
-MULT = mybir.AluOpType.mult
+MULT, ADD = mybir.AluOpType.mult, mybir.AluOpType.add
 
 P = 128
 S = 256
@@ -12,8 +13,11 @@ SIDES = M // P
 BANK = 512
 PIECE = 128
 PIECES = BANK // PIECE
-CHUNK = 256
-CHUNKS = BANK // CHUNK
+REPLICAS = 16 // SIDES
+GROUPS = P // REPLICAS
+BLOCK = N // REPLICAS
+BLOCKS = BANK // BLOCK
+STORE = 2 * BLOCK
 
 FLOPS = 2 * (2 * P) * M * N + 2 * P * M * N
 
@@ -22,8 +26,8 @@ def tile_attentionsheaflearner_kernel(tc, table, x_dst, w_src, w_dst, grp, diag,
     nc = tc.nc
     with (
         tc.tile_pool(name="held", bufs=1) as held,
-        tc.tile_pool(name="work", bufs=N // CHUNK) as work,
         tc.psum_pool(name="psum", bufs=1) as psum,
+        tc.psum_pool(name="rotating", bufs=3) as rotating,
     ):
         offsets = held.tile([P, N // 16], U16, name="offsets")
         nc.sync.dma_start(offsets[:], offs)
@@ -54,6 +58,26 @@ def tile_attentionsheaflearner_kernel(tc, table, x_dst, w_src, w_dst, grp, diag,
             nc.scalar.dma_start(grp_rows[rows, :], grp.rearrange("(q two) r -> two q r", two=2)[0])
             nc.vector.tensor_copy(grp_side[rows, rows], grp_rows[:].rearrange("q (r two) -> q two r", two=2)[rows, 0, :])
 
+        by_replica = [P, REPLICAS, GROUPS, REPLICAS]
+        diagonal = held.tile([P, REPLICAS * (REPLICAS + 1)], BF16, name="diagonal")
+        nc.vector.memset(diagonal[:], 0.0)
+        nc.vector.memset(diagonal[:].rearrange("p (r step) -> p r step", step=REPLICAS + 1)[:, :, 0], 1.0)
+        same_replica = diagonal[:, 0 : REPLICAS * REPLICAS].rearrange("p (r q) -> p r q", q=REPLICAS)
+        spread = held.tile([P, REPLICAS, P], BF16, name="spread")
+        nc.vector.tensor_tensor(
+            spread[:].rearrange("p r (a q) -> p r a q", q=REPLICAS),
+            grp_side[:].rearrange("p (a q) -> p a q", q=REPLICAS).unsqueeze(1).to_broadcast(by_replica),
+            same_replica.unsqueeze(2).to_broadcast(by_replica),
+            MULT,
+        )
+        ident = held.tile([P, P], F32, name="ident")
+        make_identity(nc, ident[:])
+        collect = held.tile([P, REPLICAS, P], F32, name="collect")
+        nc.vector.tensor_copy(
+            collect[:].rearrange("p r (a q) -> p r a q", q=REPLICAS),
+            ident[:].rearrange("p (a r) -> p r a", r=REPLICAS).unsqueeze(3).to_broadcast(by_replica),
+        )
+
         banks = range(N // BANK)
         maps = [[psum.tile([P, BANK], F32, name=f"maps{b}{side}") for side in range(SIDES)] for b in banks]
         for b in banks:
@@ -69,27 +93,42 @@ def tile_attentionsheaflearner_kernel(tc, table, x_dst, w_src, w_dst, grp, diag,
                         stop=False,
                     )
 
-        den = [psum.tile([P, CHUNK], F32, name=f"den{c}") for c in range(N // CHUNK)]
+        e_bf = [held.tile([P, N], BF16, name=f"e_bf{side}") for side in range(SIDES)]
+        e = held.tile([P, SIDES, N], F32, name="e")
+        den = psum.tile([P, BLOCK], F32, name="den")
+        for b in banks:
+            cols = slice(b * BANK, (b + 1) * BANK)
+            for side in range(SIDES):
+                nc.tensor.matmul(maps[b][side][:], w_dst_side[:, side, :], x_dst_sb[:, cols], start=False, stop=True)
+                nc.scalar.activation(e_bf[side][:, cols], maps[b][side][:], EXP)
+            for r in range(b * BLOCKS, (b + 1) * BLOCKS):
+                for side in range(SIDES):
+                    nc.tensor.matmul(
+                        den[:],
+                        spread[:, r, :],
+                        e_bf[side][:, r * BLOCK : (r + 1) * BLOCK],
+                        start=(r == 0 and side == 0),
+                        stop=(r == REPLICAS - 1 and side == SIDES - 1),
+                    )
         for b in banks:
             for side in range(SIDES):
-                nc.tensor.matmul(
-                    maps[b][side][:], w_dst_side[:, side, :], x_dst_sb[:, b * BANK : (b + 1) * BANK], start=False, stop=True
-                )
-            for c in range(b * CHUNKS, (b + 1) * CHUNKS):
-                for side in range(SIDES):
-                    e_bf = work.tile([P, CHUNK], BF16, name=f"e_bf{side}")
-                    nc.scalar.activation(e_bf[:], maps[b][side][:, (c - b * CHUNKS) * CHUNK : (c - b * CHUNKS + 1) * CHUNK], EXP)
-                    nc.tensor.matmul(den[c][:], grp_side[:], e_bf[:], start=(side == 0), stop=(side == SIDES - 1))
+                nc.scalar.activation(e[:, side, b * BANK : (b + 1) * BANK], maps[b][side][:], EXP)
 
-        for c in range(N // CHUNK):
-            b = c // CHUNKS
-            rden = work.tile([P, CHUNK], F32, name="rden")
-            nc.vector.reciprocal(rden[:], den[c][:])
-            for side in range(SIDES):
-                e = work.tile([P, CHUNK], F32, name=f"e{side}")
-                nc.scalar.activation(e[:], maps[b][side][:, (c - b * CHUNKS) * CHUNK : (c - b * CHUNKS + 1) * CHUNK], EXP)
-                share = work.tile([P, CHUNK], F32, name=f"share{side}")
-                nc.gpsimd.tensor_tensor(share[:], e[:], rden[:], MULT)
-                res = work.tile([P, CHUNK], F32, name=f"res{side}")
-                nc.scalar.activation(res[:], share[:], IDENTITY, bias=diag_sb[side][:], scale=-1.0)
-                nc.sync.dma_start(out_side[side, :, c * CHUNK : (c + 1) * CHUNK], res[:])
+        rden = held.tile([P, BLOCK], F32, name="rden")
+        nc.vector.reciprocal(rden[:], den[:])
+
+        share = held.tile([P, SIDES, N], F32, name="share")
+        res = held.tile([P, SIDES, N], F32, name="res")
+        for r in range(REPLICAS):
+            block = slice(r * BLOCK, (r + 1) * BLOCK)
+            rden_all = rotating.tile([P, BLOCK], F32, name="rden_all")
+            nc.tensor.matmul(rden_all[:], collect[:, r, :], rden[:], start=True, stop=True)
+            nc.vector.tensor_tensor(
+                share[:, :, block], e[:, :, block], rden_all[:].unsqueeze(1).to_broadcast([P, SIDES, BLOCK]), MULT
+            )
+            if (r + 1) * BLOCK % STORE == 0:
+                done = slice((r + 1) * BLOCK - STORE, (r + 1) * BLOCK)
+                nc.scalar.activation(res[:, 0, done], share[:, 0, done], IDENTITY, bias=diag_sb[0][:], scale=-1.0)
+                nc.gpsimd.tensor_scalar(res[:, 1, done], share[:, 1, done], -1.0, diag_sb[1][:], MULT, ADD)
+                for side in range(SIDES):
+                    nc.sync.dma_start(out_side[side, :, done], res[:, side, done])

@@ -3,7 +3,7 @@ from concourse.masks import make_identity
 
 BF16, F32, U16 = mybir.dt.bfloat16, mybir.dt.float32, mybir.dt.uint16
 EXP, IDENTITY = mybir.ActivationFunctionType.Exp, mybir.ActivationFunctionType.Identity
-MULT, ADD = mybir.AluOpType.mult, mybir.AluOpType.add
+MULT, ADD, SUBTRACT = mybir.AluOpType.mult, mybir.AluOpType.add, mybir.AluOpType.subtract
 
 P = 128
 S = 256
@@ -18,6 +18,7 @@ GROUPS = P // REPLICAS
 BLOCK = N // REPLICAS
 BLOCKS = BANK // BLOCK
 STORE = 2 * BLOCK
+WARM_UP = 4
 
 FLOPS = 2 * (2 * P) * M * N + 2 * P * M * N
 
@@ -26,37 +27,44 @@ def tile_attentionsheaflearner_kernel(tc, table, x_dst, w_src, w_dst, grp, diag,
     nc = tc.nc
     with (
         tc.tile_pool(name="held", bufs=1) as held,
+        tc.tile_pool(name="work", bufs=N // STORE) as work,
         tc.psum_pool(name="psum", bufs=1) as psum,
         tc.psum_pool(name="rotating", bufs=3) as rotating,
     ):
+        zeros = held.tile([P, BANK], BF16, name="zeros")
+        nc.vector.memset(zeros[:], 0.0)
+        for w in range(WARM_UP):
+            unread = rotating.tile([P, BANK], F32, name="unread", tag="rden_all")
+            nc.tensor.matmul(unread[:], zeros[:, 0:P], zeros[:], start=True, stop=True)
+
+        x_dst_sb = held.tile([P, N], BF16, name="x_dst_sb")
+        nc.sync.dma_start(x_dst_sb[:], x_dst)
+        w_dst_sb = held.tile([P, M], BF16, name="w_dst_sb")
+        nc.scalar.dma_start(w_dst_sb[:], w_dst)
+        w_src_sb = held.tile([P, M], BF16, name="w_src_sb")
+        nc.scalar.dma_start(w_src_sb[:], w_src)
         offsets = held.tile([P, N // 16], U16, name="offsets")
         nc.sync.dma_start(offsets[:], offs)
         table_sb = held.tile([P, S], BF16, name="table_sb")
         nc.sync.dma_start(table_sb[:], table)
-        w_src_sb = held.tile([P, M], BF16, name="w_src_sb")
-        nc.scalar.dma_start(w_src_sb[:], w_src)
-        w_dst_sb = held.tile([P, M], BF16, name="w_dst_sb")
-        nc.scalar.dma_start(w_dst_sb[:], w_dst)
-        x_dst_sb = held.tile([P, N], BF16, name="x_dst_sb")
-        nc.sync.dma_start(x_dst_sb[:], x_dst)
 
-        w_src_side = held.tile([P, SIDES, P], BF16, name="w_src_side")
-        nc.vector.tensor_copy(w_src_side[:], w_src_sb[:].rearrange("d (p side) -> d side p", side=SIDES))
         w_dst_side = held.tile([P, SIDES, P], BF16, name="w_dst_side")
         nc.vector.tensor_copy(w_dst_side[:], w_dst_sb[:].rearrange("d (p side) -> d side p", side=SIDES))
+        w_src_side = held.tile([P, SIDES, P], BF16, name="w_src_side")
+        nc.vector.tensor_copy(w_src_side[:], w_src_sb[:].rearrange("d (p side) -> d side p", side=SIDES))
         out_side = out.rearrange("(p side) j -> side p j", side=SIDES)
         diag_side = diag.rearrange("(p side) one -> side p one", side=SIDES)
         diag_sb = [held.tile([P, 1], F32, name=f"diag_sb{side}") for side in range(SIDES)]
-        for side in range(SIDES):
-            nc.scalar.dma_start(diag_sb[side][:], diag_side[side])
 
         grp_rows = held.tile([P, P], BF16, name="grp_rows")
         grp_side = held.tile([P, P], BF16, name="grp_side")
         nc.vector.memset(grp_side[:], 0.0)
         for half in range(2):
             rows = slice(half * (P // 2), (half + 1) * (P // 2))
-            nc.scalar.dma_start(grp_rows[rows, :], grp.rearrange("(q two) r -> two q r", two=2)[0])
+            nc.sync.dma_start(grp_rows[rows, :], grp.rearrange("(q two) r -> two q r", two=2)[0])
             nc.vector.tensor_copy(grp_side[rows, rows], grp_rows[:].rearrange("q (r two) -> q two r", two=2)[rows, 0, :])
+        for side in range(SIDES):
+            nc.sync.dma_start(diag_sb[side][:], diag_side[side])
 
         by_replica = [P, REPLICAS, GROUPS, REPLICAS]
         diagonal = held.tile([P, REPLICAS * (REPLICAS + 1)], BF16, name="diagonal")
@@ -70,9 +78,9 @@ def tile_attentionsheaflearner_kernel(tc, table, x_dst, w_src, w_dst, grp, diag,
             same_replica.unsqueeze(2).to_broadcast(by_replica),
             MULT,
         )
-        ident = held.tile([P, P], F32, name="ident")
+        ident = held.tile([P, P], BF16, name="ident")
         make_identity(nc, ident[:])
-        collect = held.tile([P, REPLICAS, P], F32, name="collect")
+        collect = held.tile([P, REPLICAS, P], BF16, name="collect")
         nc.vector.tensor_copy(
             collect[:].rearrange("p r (a q) -> p r a q", q=REPLICAS),
             ident[:].rearrange("p (a r) -> p r a", r=REPLICAS).unsqueeze(3).to_broadcast(by_replica),
@@ -82,6 +90,11 @@ def tile_attentionsheaflearner_kernel(tc, table, x_dst, w_src, w_dst, grp, diag,
         maps = [[psum.tile([P, BANK], F32, name=f"maps{b}{side}") for side in range(SIDES)] for b in banks]
         for b in banks:
             for side in range(SIDES):
+                nc.tensor.matmul(
+                    maps[b][side][:], w_dst_side[:, side, :], x_dst_sb[:, b * BANK : (b + 1) * BANK], start=True, stop=False
+                )
+        for b in banks:
+            for side in range(SIDES):
                 for k in range(PIECES):
                     piece = b * PIECES + k
                     looked_up = table_sb[:].indirect(offsets[:, piece * (PIECE // 16) : (piece + 1) * (PIECE // 16)])
@@ -89,18 +102,16 @@ def tile_attentionsheaflearner_kernel(tc, table, x_dst, w_src, w_dst, grp, diag,
                         maps[b][side][:, k * PIECE : (k + 1) * PIECE],
                         w_src_side[:, side, :],
                         looked_up,
-                        start=(k == 0),
-                        stop=False,
+                        start=False,
+                        stop=(k == PIECES - 1),
                     )
 
         e_bf = [held.tile([P, N], BF16, name=f"e_bf{side}") for side in range(SIDES)]
-        e = held.tile([P, SIDES, N], F32, name="e")
+        e = [held.tile([P, SIDES, BANK], F32, name=f"e{b}") for b in banks]
         den = psum.tile([P, BLOCK], F32, name="den")
         for b in banks:
-            cols = slice(b * BANK, (b + 1) * BANK)
             for side in range(SIDES):
-                nc.tensor.matmul(maps[b][side][:], w_dst_side[:, side, :], x_dst_sb[:, cols], start=False, stop=True)
-                nc.scalar.activation(e_bf[side][:, cols], maps[b][side][:], EXP)
+                nc.scalar.activation(e_bf[side][:, b * BANK : (b + 1) * BANK], maps[b][side][:], EXP)
             for r in range(b * BLOCKS, (b + 1) * BLOCKS):
                 for side in range(SIDES):
                     nc.tensor.matmul(
@@ -112,23 +123,32 @@ def tile_attentionsheaflearner_kernel(tc, table, x_dst, w_src, w_dst, grp, diag,
                     )
         for b in banks:
             for side in range(SIDES):
-                nc.scalar.activation(e[:, side, b * BANK : (b + 1) * BANK], maps[b][side][:], EXP)
+                nc.scalar.activation(e[b][:, side, :], maps[b][side][:], EXP)
 
         rden = held.tile([P, BLOCK], F32, name="rden")
         nc.vector.reciprocal(rden[:], den[:])
+        rden_hi = held.tile([P, BLOCK], BF16, name="rden_hi")
+        nc.vector.tensor_copy(rden_hi[:], rden[:])
+        rden_lo = held.tile([P, BLOCK], BF16, name="rden_lo")
+        nc.vector.tensor_tensor(rden_lo[:], rden[:], rden_hi[:], SUBTRACT)
 
-        share = held.tile([P, SIDES, N], F32, name="share")
-        res = held.tile([P, SIDES, N], F32, name="res")
-        for r in range(REPLICAS):
-            block = slice(r * BLOCK, (r + 1) * BLOCK)
-            rden_all = rotating.tile([P, BLOCK], F32, name="rden_all")
-            nc.tensor.matmul(rden_all[:], collect[:, r, :], rden[:], start=True, stop=True)
+        for c in range(N // STORE):
+            b = c * STORE // BANK
+            rden_all = rotating.tile([P, STORE], F32, name="rden_all")
+            for i in range(STORE // BLOCK):
+                r = c * (STORE // BLOCK) + i
+                here = rden_all[:, i * BLOCK : (i + 1) * BLOCK]
+                nc.tensor.matmul(here, collect[:, r, :], rden_hi[:], start=True, stop=False)
+                nc.tensor.matmul(here, collect[:, r, :], rden_lo[:], start=False, stop=True)
+            share = work.tile([P, SIDES, STORE], F32, name="share")
             nc.vector.tensor_tensor(
-                share[:, :, block], e[:, :, block], rden_all[:].unsqueeze(1).to_broadcast([P, SIDES, BLOCK]), MULT
+                share[:],
+                e[b][:, :, c * STORE - b * BANK : (c + 1) * STORE - b * BANK],
+                rden_all[:].unsqueeze(1).to_broadcast([P, SIDES, STORE]),
+                MULT,
             )
-            if (r + 1) * BLOCK % STORE == 0:
-                done = slice((r + 1) * BLOCK - STORE, (r + 1) * BLOCK)
-                nc.scalar.activation(res[:, 0, done], share[:, 0, done], IDENTITY, bias=diag_sb[0][:], scale=-1.0)
-                nc.gpsimd.tensor_scalar(res[:, 1, done], share[:, 1, done], -1.0, diag_sb[1][:], MULT, ADD)
-                for side in range(SIDES):
-                    nc.sync.dma_start(out_side[side, :, done], res[:, side, done])
+            res = [work.tile([P, STORE], F32, name=f"res{side}") for side in range(SIDES)]
+            nc.scalar.activation(res[0][:], share[:, 0, :], IDENTITY, bias=diag_sb[0][:], scale=-1.0)
+            nc.gpsimd.tensor_scalar(res[1][:], share[:, 1, :], -1.0, diag_sb[1][:], MULT, ADD)
+            for side in range(SIDES):
+                nc.sync.dma_start(out_side[side, :, c * STORE : (c + 1) * STORE], res[side][:])

@@ -3,7 +3,7 @@ from concourse.masks import make_identity
 
 BF16, F32, U16 = mybir.dt.bfloat16, mybir.dt.float32, mybir.dt.uint16
 EXP, IDENTITY = mybir.ActivationFunctionType.Exp, mybir.ActivationFunctionType.Identity
-MULT, ADD, SUBTRACT = mybir.AluOpType.mult, mybir.AluOpType.add, mybir.AluOpType.subtract
+MULT, ADD = mybir.AluOpType.mult, mybir.AluOpType.add
 
 P = 128
 S = 256
@@ -27,7 +27,6 @@ def tile_attentionsheaflearner_kernel(tc, table, x_dst, w_src, w_dst, grp, diag,
     nc = tc.nc
     with (
         tc.tile_pool(name="held", bufs=1) as held,
-        tc.tile_pool(name="work", bufs=N // STORE) as work,
         tc.psum_pool(name="psum", bufs=1) as psum,
         tc.psum_pool(name="rotating", bufs=3) as rotating,
     ):
@@ -37,34 +36,34 @@ def tile_attentionsheaflearner_kernel(tc, table, x_dst, w_src, w_dst, grp, diag,
             unread = rotating.tile([P, BANK], F32, name="unread", tag="rden_all")
             nc.tensor.matmul(unread[:], zeros[:, 0:P], zeros[:], start=True, stop=True)
 
-        x_dst_sb = held.tile([P, N], BF16, name="x_dst_sb")
-        nc.sync.dma_start(x_dst_sb[:], x_dst)
-        w_dst_sb = held.tile([P, M], BF16, name="w_dst_sb")
-        nc.scalar.dma_start(w_dst_sb[:], w_dst)
-        w_src_sb = held.tile([P, M], BF16, name="w_src_sb")
-        nc.scalar.dma_start(w_src_sb[:], w_src)
         offsets = held.tile([P, N // 16], U16, name="offsets")
         nc.sync.dma_start(offsets[:], offs)
         table_sb = held.tile([P, S], BF16, name="table_sb")
         nc.sync.dma_start(table_sb[:], table)
+        w_src_sb = held.tile([P, M], BF16, name="w_src_sb")
+        nc.scalar.dma_start(w_src_sb[:], w_src)
+        w_dst_sb = held.tile([P, M], BF16, name="w_dst_sb")
+        nc.scalar.dma_start(w_dst_sb[:], w_dst)
+        x_dst_sb = held.tile([P, N], BF16, name="x_dst_sb")
+        nc.sync.dma_start(x_dst_sb[:], x_dst)
 
-        w_dst_side = held.tile([P, SIDES, P], BF16, name="w_dst_side")
-        nc.vector.tensor_copy(w_dst_side[:], w_dst_sb[:].rearrange("d (p side) -> d side p", side=SIDES))
         w_src_side = held.tile([P, SIDES, P], BF16, name="w_src_side")
         nc.vector.tensor_copy(w_src_side[:], w_src_sb[:].rearrange("d (p side) -> d side p", side=SIDES))
+        w_dst_side = held.tile([P, SIDES, P], BF16, name="w_dst_side")
+        nc.vector.tensor_copy(w_dst_side[:], w_dst_sb[:].rearrange("d (p side) -> d side p", side=SIDES))
         out_side = out.rearrange("(p side) j -> side p j", side=SIDES)
         diag_side = diag.rearrange("(p side) one -> side p one", side=SIDES)
         diag_sb = [held.tile([P, 1], F32, name=f"diag_sb{side}") for side in range(SIDES)]
+        for side in range(SIDES):
+            nc.scalar.dma_start(diag_sb[side][:], diag_side[side])
 
         grp_rows = held.tile([P, P], BF16, name="grp_rows")
         grp_side = held.tile([P, P], BF16, name="grp_side")
         nc.vector.memset(grp_side[:], 0.0)
         for half in range(2):
             rows = slice(half * (P // 2), (half + 1) * (P // 2))
-            nc.sync.dma_start(grp_rows[rows, :], grp.rearrange("(q two) r -> two q r", two=2)[0])
+            nc.scalar.dma_start(grp_rows[rows, :], grp.rearrange("(q two) r -> two q r", two=2)[0])
             nc.vector.tensor_copy(grp_side[rows, rows], grp_rows[:].rearrange("q (r two) -> q two r", two=2)[rows, 0, :])
-        for side in range(SIDES):
-            nc.sync.dma_start(diag_sb[side][:], diag_side[side])
 
         by_replica = [P, REPLICAS, GROUPS, REPLICAS]
         diagonal = held.tile([P, REPLICAS * (REPLICAS + 1)], BF16, name="diagonal")
@@ -78,9 +77,9 @@ def tile_attentionsheaflearner_kernel(tc, table, x_dst, w_src, w_dst, grp, diag,
             same_replica.unsqueeze(2).to_broadcast(by_replica),
             MULT,
         )
-        ident = held.tile([P, P], BF16, name="ident")
+        ident = held.tile([P, P], F32, name="ident")
         make_identity(nc, ident[:])
-        collect = held.tile([P, REPLICAS, P], BF16, name="collect")
+        collect = held.tile([P, REPLICAS, P], F32, name="collect")
         nc.vector.tensor_copy(
             collect[:].rearrange("p r (a q) -> p r a q", q=REPLICAS),
             ident[:].rearrange("p (a r) -> p r a", r=REPLICAS).unsqueeze(3).to_broadcast(by_replica),
@@ -90,11 +89,6 @@ def tile_attentionsheaflearner_kernel(tc, table, x_dst, w_src, w_dst, grp, diag,
         maps = [[psum.tile([P, BANK], F32, name=f"maps{b}{side}") for side in range(SIDES)] for b in banks]
         for b in banks:
             for side in range(SIDES):
-                nc.tensor.matmul(
-                    maps[b][side][:], w_dst_side[:, side, :], x_dst_sb[:, b * BANK : (b + 1) * BANK], start=True, stop=False
-                )
-        for b in banks:
-            for side in range(SIDES):
                 for k in range(PIECES):
                     piece = b * PIECES + k
                     looked_up = table_sb[:].indirect(offsets[:, piece * (PIECE // 16) : (piece + 1) * (PIECE // 16)])
@@ -102,16 +96,18 @@ def tile_attentionsheaflearner_kernel(tc, table, x_dst, w_src, w_dst, grp, diag,
                         maps[b][side][:, k * PIECE : (k + 1) * PIECE],
                         w_src_side[:, side, :],
                         looked_up,
-                        start=False,
-                        stop=(k == PIECES - 1),
+                        start=(k == 0),
+                        stop=False,
                     )
 
         e_bf = [held.tile([P, N], BF16, name=f"e_bf{side}") for side in range(SIDES)]
-        e = [held.tile([P, SIDES, BANK], F32, name=f"e{b}") for b in banks]
+        e = held.tile([P, SIDES, N], F32, name="e")
         den = psum.tile([P, BLOCK], F32, name="den")
         for b in banks:
+            cols = slice(b * BANK, (b + 1) * BANK)
             for side in range(SIDES):
-                nc.scalar.activation(e_bf[side][:, b * BANK : (b + 1) * BANK], maps[b][side][:], EXP)
+                nc.tensor.matmul(maps[b][side][:], w_dst_side[:, side, :], x_dst_sb[:, cols], start=False, stop=True)
+                nc.scalar.activation(e_bf[side][:, cols], maps[b][side][:], EXP)
             for r in range(b * BLOCKS, (b + 1) * BLOCKS):
                 for side in range(SIDES):
                     nc.tensor.matmul(
@@ -123,32 +119,23 @@ def tile_attentionsheaflearner_kernel(tc, table, x_dst, w_src, w_dst, grp, diag,
                     )
         for b in banks:
             for side in range(SIDES):
-                nc.scalar.activation(e[b][:, side, :], maps[b][side][:], EXP)
+                nc.scalar.activation(e[:, side, b * BANK : (b + 1) * BANK], maps[b][side][:], EXP)
 
         rden = held.tile([P, BLOCK], F32, name="rden")
         nc.vector.reciprocal(rden[:], den[:])
-        rden_hi = held.tile([P, BLOCK], BF16, name="rden_hi")
-        nc.vector.tensor_copy(rden_hi[:], rden[:])
-        rden_lo = held.tile([P, BLOCK], BF16, name="rden_lo")
-        nc.vector.tensor_tensor(rden_lo[:], rden[:], rden_hi[:], SUBTRACT)
 
-        for c in range(N // STORE):
-            b = c * STORE // BANK
-            rden_all = rotating.tile([P, STORE], F32, name="rden_all")
-            for i in range(STORE // BLOCK):
-                r = c * (STORE // BLOCK) + i
-                here = rden_all[:, i * BLOCK : (i + 1) * BLOCK]
-                nc.tensor.matmul(here, collect[:, r, :], rden_hi[:], start=True, stop=False)
-                nc.tensor.matmul(here, collect[:, r, :], rden_lo[:], start=False, stop=True)
-            share = work.tile([P, SIDES, STORE], F32, name="share")
+        share = held.tile([P, SIDES, N], F32, name="share")
+        res = held.tile([P, SIDES, N], F32, name="res")
+        for r in range(REPLICAS):
+            block = slice(r * BLOCK, (r + 1) * BLOCK)
+            rden_all = rotating.tile([P, BLOCK], F32, name="rden_all")
+            nc.tensor.matmul(rden_all[:], collect[:, r, :], rden[:], start=True, stop=True)
             nc.vector.tensor_tensor(
-                share[:],
-                e[b][:, :, c * STORE - b * BANK : (c + 1) * STORE - b * BANK],
-                rden_all[:].unsqueeze(1).to_broadcast([P, SIDES, STORE]),
-                MULT,
+                share[:, :, block], e[:, :, block], rden_all[:].unsqueeze(1).to_broadcast([P, SIDES, BLOCK]), MULT
             )
-            res = [work.tile([P, STORE], F32, name=f"res{side}") for side in range(SIDES)]
-            nc.scalar.activation(res[0][:], share[:, 0, :], IDENTITY, bias=diag_sb[0][:], scale=-1.0)
-            nc.gpsimd.tensor_scalar(res[1][:], share[:, 1, :], -1.0, diag_sb[1][:], MULT, ADD)
-            for side in range(SIDES):
-                nc.sync.dma_start(out_side[side, :, c * STORE : (c + 1) * STORE], res[side][:])
+            if (r + 1) * BLOCK % STORE == 0:
+                done = slice((r + 1) * BLOCK - STORE, (r + 1) * BLOCK)
+                nc.scalar.activation(res[:, 0, done], share[:, 0, done], IDENTITY, bias=diag_sb[0][:], scale=-1.0)
+                nc.gpsimd.tensor_scalar(res[:, 1, done], share[:, 1, done], -1.0, diag_sb[1][:], MULT, ADD)
+                for side in range(SIDES):
+                    nc.sync.dma_start(out_side[side, :, done], res[:, side, done])

@@ -10,15 +10,13 @@ S = 256
 N = 1024
 M = 256
 SIDES = M // P
-BANK = 512
-PIECE = 128
-PIECES = BANK // PIECE
+PIECE = 256
+PIECES = N // PIECE
+PSUM_BANKS = 8
 REPLICAS = 16 // SIDES
 GROUPS = P // REPLICAS
 BLOCK = N // REPLICAS
-BLOCKS = BANK // BLOCK
-STORE = 2 * BLOCK
-WARM_UP = 4
+BLOCKS = PIECE // BLOCK
 
 FLOPS = 2 * (2 * P) * M * N + 2 * P * M * N
 
@@ -27,15 +25,9 @@ def tile_attentionsheaflearner_kernel(tc, table, x_dst, w_src, w_dst, grp, diag,
     nc = tc.nc
     with (
         tc.tile_pool(name="held", bufs=1) as held,
-        tc.psum_pool(name="psum", bufs=1) as psum,
-        tc.psum_pool(name="rotating", bufs=3) as rotating,
+        tc.tile_pool(name="work", bufs=PIECES) as work,
+        tc.psum_pool(name="psum", bufs=PSUM_BANKS) as psum,
     ):
-        zeros = held.tile([P, BANK], BF16, name="zeros")
-        nc.vector.memset(zeros[:], 0.0)
-        for w in range(WARM_UP):
-            unread = rotating.tile([P, BANK], F32, name="unread", tag="rden_all")
-            nc.tensor.matmul(unread[:], zeros[:, 0:P], zeros[:], start=True, stop=True)
-
         offsets = held.tile([P, N // 16], U16, name="offsets")
         nc.sync.dma_start(offsets[:], offs)
         table_sb = held.tile([P, S], BF16, name="table_sb")
@@ -53,9 +45,6 @@ def tile_attentionsheaflearner_kernel(tc, table, x_dst, w_src, w_dst, grp, diag,
         nc.vector.tensor_copy(w_dst_side[:], w_dst_sb[:].rearrange("d (p side) -> d side p", side=SIDES))
         out_side = out.rearrange("(p side) j -> side p j", side=SIDES)
         diag_side = diag.rearrange("(p side) one -> side p one", side=SIDES)
-        diag_sb = [held.tile([P, 1], F32, name=f"diag_sb{side}") for side in range(SIDES)]
-        for side in range(SIDES):
-            nc.scalar.dma_start(diag_sb[side][:], diag_side[side])
 
         grp_rows = held.tile([P, P], BF16, name="grp_rows")
         grp_side = held.tile([P, P], BF16, name="grp_side")
@@ -64,6 +53,9 @@ def tile_attentionsheaflearner_kernel(tc, table, x_dst, w_src, w_dst, grp, diag,
             rows = slice(half * (P // 2), (half + 1) * (P // 2))
             nc.scalar.dma_start(grp_rows[rows, :], grp.rearrange("(q two) r -> two q r", two=2)[0])
             nc.vector.tensor_copy(grp_side[rows, rows], grp_rows[:].rearrange("q (r two) -> q two r", two=2)[rows, 0, :])
+        diag_sb = [held.tile([P, 1], F32, name=f"diag_sb{side}") for side in range(SIDES)]
+        for side in range(SIDES):
+            nc.scalar.dma_start(diag_sb[side][:], diag_side[side])
 
         by_replica = [P, REPLICAS, GROUPS, REPLICAS]
         diagonal = held.tile([P, REPLICAS * (REPLICAS + 1)], BF16, name="diagonal")
@@ -85,57 +77,49 @@ def tile_attentionsheaflearner_kernel(tc, table, x_dst, w_src, w_dst, grp, diag,
             ident[:].rearrange("p (a r) -> p r a", r=REPLICAS).unsqueeze(3).to_broadcast(by_replica),
         )
 
-        banks = range(N // BANK)
-        maps = [[psum.tile([P, BANK], F32, name=f"maps{b}{side}") for side in range(SIDES)] for b in banks]
-        for b in banks:
+        maps = [[psum.tile([P, PIECE], F32, name=f"maps{c}{side}", tag="bank") for side in range(SIDES)] for c in range(PIECES)]
+        for c in range(PIECES):
+            looked_up = table_sb[:].indirect(offsets[:, c * (PIECE // 16) : (c + 1) * (PIECE // 16)])
             for side in range(SIDES):
-                for k in range(PIECES):
-                    piece = b * PIECES + k
-                    looked_up = table_sb[:].indirect(offsets[:, piece * (PIECE // 16) : (piece + 1) * (PIECE // 16)])
-                    nc.tensor.matmul(
-                        maps[b][side][:, k * PIECE : (k + 1) * PIECE],
-                        w_src_side[:, side, :],
-                        looked_up,
-                        start=(k == 0),
-                        stop=False,
-                    )
+                nc.tensor.matmul(maps[c][side][:], w_src_side[:, side, :], looked_up, start=True, stop=False)
+        for c in range(PIECES):
+            for side in range(SIDES):
+                nc.tensor.matmul(
+                    maps[c][side][:], w_dst_side[:, side, :], x_dst_sb[:, c * PIECE : (c + 1) * PIECE], start=False, stop=True
+                )
 
-        e_bf = [held.tile([P, N], BF16, name=f"e_bf{side}") for side in range(SIDES)]
-        e = held.tile([P, SIDES, N], F32, name="e")
-        den = psum.tile([P, BLOCK], F32, name="den")
-        for b in banks:
-            cols = slice(b * BANK, (b + 1) * BANK)
+        e = [held.tile([P, SIDES, PIECE], F32, name=f"e{c}") for c in range(PIECES)]
+        e_bf = [held.tile([P, SIDES, PIECE], BF16, name=f"e_bf{c}") for c in range(PIECES)]
+        for c in range(PIECES):
             for side in range(SIDES):
-                nc.tensor.matmul(maps[b][side][:], w_dst_side[:, side, :], x_dst_sb[:, cols], start=False, stop=True)
-                nc.scalar.activation(e_bf[side][:, cols], maps[b][side][:], EXP)
-            for r in range(b * BLOCKS, (b + 1) * BLOCKS):
-                for side in range(SIDES):
-                    nc.tensor.matmul(
-                        den[:],
-                        spread[:, r, :],
-                        e_bf[side][:, r * BLOCK : (r + 1) * BLOCK],
-                        start=(r == 0 and side == 0),
-                        stop=(r == REPLICAS - 1 and side == SIDES - 1),
-                    )
-        for b in banks:
+                nc.scalar.activation(e[c][:, side, :], maps[c][side][:], EXP)
+                nc.vector.tensor_copy(e_bf[c][:, side, :], e[c][:, side, :])
+        den = psum.tile([P, BLOCK], F32, name="den", tag="bank")
+        for r in range(REPLICAS):
+            c = r // BLOCKS
             for side in range(SIDES):
-                nc.scalar.activation(e[:, side, b * BANK : (b + 1) * BANK], maps[b][side][:], EXP)
-
+                nc.tensor.matmul(
+                    den[:],
+                    spread[:, r, :],
+                    e_bf[c][:, side, (r - c * BLOCKS) * BLOCK : (r - c * BLOCKS + 1) * BLOCK],
+                    start=(r == 0 and side == 0),
+                    stop=(r == REPLICAS - 1 and side == SIDES - 1),
+                )
         rden = held.tile([P, BLOCK], F32, name="rden")
         nc.vector.reciprocal(rden[:], den[:])
 
-        share = held.tile([P, SIDES, N], F32, name="share")
-        res = held.tile([P, SIDES, N], F32, name="res")
-        for r in range(REPLICAS):
-            block = slice(r * BLOCK, (r + 1) * BLOCK)
-            rden_all = rotating.tile([P, BLOCK], F32, name="rden_all")
-            nc.tensor.matmul(rden_all[:], collect[:, r, :], rden[:], start=True, stop=True)
+        for c in range(PIECES):
+            rden_all = psum.tile([P, PIECE], F32, name="rden_all", tag="bank")
+            for i in range(BLOCKS):
+                nc.tensor.matmul(
+                    rden_all[:, i * BLOCK : (i + 1) * BLOCK], collect[:, c * BLOCKS + i, :], rden[:], start=True, stop=True
+                )
+            share = work.tile([P, SIDES, PIECE], F32, name="share")
             nc.vector.tensor_tensor(
-                share[:, :, block], e[:, :, block], rden_all[:].unsqueeze(1).to_broadcast([P, SIDES, BLOCK]), MULT
+                share[:], e[c][:], rden_all[:].unsqueeze(1).to_broadcast([P, SIDES, PIECE]), MULT
             )
-            if (r + 1) * BLOCK % STORE == 0:
-                done = slice((r + 1) * BLOCK - STORE, (r + 1) * BLOCK)
-                nc.scalar.activation(res[:, 0, done], share[:, 0, done], IDENTITY, bias=diag_sb[0][:], scale=-1.0)
-                nc.gpsimd.tensor_scalar(res[:, 1, done], share[:, 1, done], -1.0, diag_sb[1][:], MULT, ADD)
-                for side in range(SIDES):
-                    nc.sync.dma_start(out_side[side, :, done], res[:, side, done])
+            res = [work.tile([P, PIECE], F32, name=f"res{side}") for side in range(SIDES)]
+            nc.scalar.activation(res[0][:], share[:, 0, :], IDENTITY, bias=diag_sb[0][:], scale=-1.0)
+            nc.gpsimd.tensor_scalar(res[1][:], share[:, 1, :], -1.0, diag_sb[1][:], MULT, ADD)
+            for side in range(SIDES):
+                nc.sync.dma_start(out_side[side, :, c * PIECE : (c + 1) * PIECE], res[side][:])

@@ -2,7 +2,11 @@ import concourse.mybir as mybir
 from concourse.masks import make_identity
 
 BF16, F32, U16 = mybir.dt.bfloat16, mybir.dt.float32, mybir.dt.uint16
-EXP, IDENTITY = mybir.ActivationFunctionType.Exp, mybir.ActivationFunctionType.Identity
+EXP, COPY, IDENTITY = (
+    mybir.ActivationFunctionType.Exp,
+    mybir.ActivationFunctionType.Copy,
+    mybir.ActivationFunctionType.Identity,
+)
 MULT, ADD = mybir.AluOpType.mult, mybir.AluOpType.add
 
 P = 128
@@ -15,8 +19,7 @@ PIECES = N // PIECE
 PSUM_BANKS = 8
 REPLICAS = 16 // SIDES
 GROUPS = P // REPLICAS
-BLOCK = N // REPLICAS
-BLOCKS = PIECE // BLOCK
+BLOCKS = PIECE // P
 
 FLOPS = 2 * (2 * P) * M * N + 2 * P * M * N
 
@@ -25,7 +28,6 @@ def tile_attentionsheaflearner_kernel(tc, table, x_dst, w_src, w_dst, grp, diag,
     nc = tc.nc
     with (
         tc.tile_pool(name="held", bufs=1) as held,
-        tc.tile_pool(name="work", bufs=PIECES) as work,
         tc.psum_pool(name="psum", bufs=PSUM_BANKS) as psum,
     ):
         offsets = held.tile([P, N // 16], U16, name="offsets")
@@ -44,38 +46,21 @@ def tile_attentionsheaflearner_kernel(tc, table, x_dst, w_src, w_dst, grp, diag,
         w_dst_side = held.tile([P, SIDES, P], BF16, name="w_dst_side")
         nc.vector.tensor_copy(w_dst_side[:], w_dst_sb[:].rearrange("d (p side) -> d side p", side=SIDES))
         out_side = out.rearrange("(p side) j -> side p j", side=SIDES)
-        diag_side = diag.rearrange("(p side) one -> side p one", side=SIDES)
+        diag_sb = held.tile([P, SIDES], F32, name="diag_sb")
+        nc.scalar.dma_start(diag_sb[:], diag.rearrange("(p side) one -> p (side one)", side=SIDES))
 
         grp_rows = held.tile([P, P], BF16, name="grp_rows")
-        grp_side = held.tile([P, P], BF16, name="grp_side")
-        nc.vector.memset(grp_side[:], 0.0)
+        group_of = held.tile([P, GROUPS], BF16, name="group_of")
+        nc.vector.memset(group_of[:], 0.0)
         for half in range(2):
             rows = slice(half * (P // 2), (half + 1) * (P // 2))
             nc.scalar.dma_start(grp_rows[rows, :], grp.rearrange("(q two) r -> two q r", two=2)[0])
-            nc.vector.tensor_copy(grp_side[rows, rows], grp_rows[:].rearrange("q (r two) -> q two r", two=2)[rows, 0, :])
-        diag_sb = [held.tile([P, 1], F32, name=f"diag_sb{side}") for side in range(SIDES)]
-        for side in range(SIDES):
-            nc.scalar.dma_start(diag_sb[side][:], diag_side[side])
-
-        by_replica = [P, REPLICAS, GROUPS, REPLICAS]
-        diagonal = held.tile([P, REPLICAS * (REPLICAS + 1)], BF16, name="diagonal")
-        nc.vector.memset(diagonal[:], 0.0)
-        nc.vector.memset(diagonal[:].rearrange("p (r step) -> p r step", step=REPLICAS + 1)[:, :, 0], 1.0)
-        same_replica = diagonal[:, 0 : REPLICAS * REPLICAS].rearrange("p (r q) -> p r q", q=REPLICAS)
-        spread = held.tile([P, REPLICAS, P], BF16, name="spread")
-        nc.vector.tensor_tensor(
-            spread[:].rearrange("p r (a q) -> p r a q", q=REPLICAS),
-            grp_side[:].rearrange("p (a q) -> p a q", q=REPLICAS).unsqueeze(1).to_broadcast(by_replica),
-            same_replica.unsqueeze(2).to_broadcast(by_replica),
-            MULT,
-        )
+            nc.vector.tensor_copy(
+                group_of[rows, half * (GROUPS // 2) : (half + 1) * (GROUPS // 2)],
+                grp_rows[:].rearrange("q (a b) -> q b a", b=16)[rows, 0, :],
+            )
         ident = held.tile([P, P], F32, name="ident")
         make_identity(nc, ident[:])
-        collect = held.tile([P, REPLICAS, P], F32, name="collect")
-        nc.vector.tensor_copy(
-            collect[:].rearrange("p r (a q) -> p r a q", q=REPLICAS),
-            ident[:].rearrange("p (a r) -> p r a", r=REPLICAS).unsqueeze(3).to_broadcast(by_replica),
-        )
 
         maps = [[psum.tile([P, PIECE], F32, name=f"maps{c}{side}", tag="bank") for side in range(SIDES)] for c in range(PIECES)]
         for c in range(PIECES):
@@ -90,36 +75,49 @@ def tile_attentionsheaflearner_kernel(tc, table, x_dst, w_src, w_dst, grp, diag,
 
         e = [held.tile([P, SIDES, PIECE], F32, name=f"e{c}") for c in range(PIECES)]
         e_bf = [held.tile([P, SIDES, PIECE], BF16, name=f"e_bf{c}") for c in range(PIECES)]
-        for c in range(PIECES):
+        rden_t = [held.tile([P, BLOCKS * GROUPS], F32, name=f"rden_t{c}") for c in range(PIECES)]
+        rden_wide = [held.tile([P, BLOCKS * P], F32, name=f"rden_wide{c}") for c in range(PIECES)]
+
+        def exponentials(c):
             for side in range(SIDES):
                 nc.scalar.activation(e[c][:, side, :], maps[c][side][:], EXP)
                 nc.vector.tensor_copy(e_bf[c][:, side, :], e[c][:, side, :])
-        den = psum.tile([P, BLOCK], F32, name="den", tag="bank")
-        for r in range(REPLICAS):
-            c = r // BLOCKS
-            for side in range(SIDES):
-                nc.tensor.matmul(
-                    den[:],
-                    spread[:, r, :],
-                    e_bf[c][:, side, (r - c * BLOCKS) * BLOCK : (r - c * BLOCKS + 1) * BLOCK],
-                    start=(r == 0 and side == 0),
-                    stop=(r == REPLICAS - 1 and side == SIDES - 1),
-                )
-        rden = held.tile([P, BLOCK], F32, name="rden")
-        nc.vector.reciprocal(rden[:], den[:])
 
-        for c in range(PIECES):
+        def reciprocals(c):
+            den_t = psum.tile([P, BLOCKS * GROUPS], F32, name="den_t", tag="bank")
+            for i in range(BLOCKS):
+                for side in range(SIDES):
+                    nc.tensor.matmul(
+                        den_t[:, i * GROUPS : (i + 1) * GROUPS],
+                        e_bf[c][:, side, i * P : (i + 1) * P],
+                        group_of[:],
+                        start=(side == 0),
+                        stop=(side == SIDES - 1),
+                    )
+            nc.vector.reciprocal(rden_t[c][:], den_t[:])
+            nc.scalar.activation(
+                rden_wide[c][:].rearrange("j (g q) -> j g q", q=REPLICAS),
+                rden_t[c][:].unsqueeze(2).to_broadcast([P, BLOCKS * GROUPS, REPLICAS]),
+                COPY,
+            )
+
+        def results(c):
             rden_all = psum.tile([P, PIECE], F32, name="rden_all", tag="bank")
             for i in range(BLOCKS):
-                nc.tensor.matmul(
-                    rden_all[:, i * BLOCK : (i + 1) * BLOCK], collect[:, c * BLOCKS + i, :], rden[:], start=True, stop=True
-                )
-            share = work.tile([P, SIDES, PIECE], F32, name="share")
+                nc.tensor.transpose(rden_all[:, i * P : (i + 1) * P], rden_wide[c][:, i * P : (i + 1) * P], ident[:])
+            share = held.tile([P, SIDES, PIECE], F32, name=f"share{c}")
             nc.vector.tensor_tensor(
                 share[:], e[c][:], rden_all[:].unsqueeze(1).to_broadcast([P, SIDES, PIECE]), MULT
             )
-            res = [work.tile([P, PIECE], F32, name=f"res{side}") for side in range(SIDES)]
-            nc.scalar.activation(res[0][:], share[:, 0, :], IDENTITY, bias=diag_sb[0][:], scale=-1.0)
-            nc.gpsimd.tensor_scalar(res[1][:], share[:, 1, :], -1.0, diag_sb[1][:], MULT, ADD)
+            res = [held.tile([P, PIECE], F32, name=f"res{c}{side}") for side in range(SIDES)]
+            nc.scalar.activation(res[0][:], share[:, 0, :], IDENTITY, bias=diag_sb[:, 0:1], scale=-1.0)
+            nc.gpsimd.tensor_scalar(res[1][:], share[:, 1, :], -1.0, diag_sb[:, 1:2], MULT, ADD)
             for side in range(SIDES):
                 nc.sync.dma_start(out_side[side, :, c * PIECE : (c + 1) * PIECE], res[side][:])
+
+        for c in range(PIECES):
+            exponentials(c)
+        for c in range(PIECES):
+            reciprocals(c)
+        for c in range(PIECES):
+            results(c)

@@ -30,21 +30,21 @@ def tile_attentionsheaflearner_kernel(tc, table, x_dst, w_src, w_dst, grp, diag,
         tc.tile_pool(name="held", bufs=1) as held,
         tc.psum_pool(name="psum", bufs=PSUM_BANKS) as psum,
     ):
-        offsets = held.tile([P, N // 16], U16, name="offsets")
-        nc.sync.dma_start(offsets[:], offs)
-        table_sb = held.tile([P, S], BF16, name="table_sb")
-        nc.sync.dma_start(table_sb[:], table)
-        w_src_sb = held.tile([P, M], BF16, name="w_src_sb")
-        nc.scalar.dma_start(w_src_sb[:], w_src)
+        x_dst_sb = held.tile([P, N], BF16, name="x_dst_sb")
+        nc.sync.dma_start(x_dst_sb[:, 0 : N // 2], x_dst[:, 0 : N // 2])
         w_dst_sb = held.tile([P, M], BF16, name="w_dst_sb")
         nc.scalar.dma_start(w_dst_sb[:], w_dst)
-        x_dst_sb = held.tile([P, N], BF16, name="x_dst_sb")
-        nc.sync.dma_start(x_dst_sb[:], x_dst)
+        offsets = held.tile([P, N // 16], U16, name="offsets")
+        nc.sync.dma_start(offsets[:], offs)
+        w_src_sb = held.tile([P, M], BF16, name="w_src_sb")
+        nc.scalar.dma_start(w_src_sb[:], w_src)
+        table_sb = held.tile([P, S], BF16, name="table_sb")
+        nc.sync.dma_start(table_sb[:], table)
+        nc.sync.dma_start(x_dst_sb[:, N // 2 : N], x_dst[:, N // 2 : N])
 
         w_src_side = held.tile([P, SIDES, P], BF16, name="w_src_side")
         nc.vector.tensor_copy(w_src_side[:], w_src_sb[:].rearrange("d (p side) -> d side p", side=SIDES))
-        w_dst_side = held.tile([P, SIDES, P], BF16, name="w_dst_side")
-        nc.vector.tensor_copy(w_dst_side[:], w_dst_sb[:].rearrange("d (p side) -> d side p", side=SIDES))
+        w_dst_side = w_dst_sb[:].rearrange("d (p side) -> d side p", side=SIDES)
         out_side = out.rearrange("(p side) j -> side p j", side=SIDES)
         diag_sb = held.tile([P, SIDES], F32, name="diag_sb")
         nc.scalar.dma_start(diag_sb[:], diag.rearrange("(p side) one -> p (side one)", side=SIDES))
@@ -63,15 +63,29 @@ def tile_attentionsheaflearner_kernel(tc, table, x_dst, w_src, w_dst, grp, diag,
         make_identity(nc, ident[:])
 
         maps = [[psum.tile([P, PIECE], F32, name=f"maps{c}{side}", tag="bank") for side in range(SIDES)] for c in range(PIECES)]
+        plain_first = range(PIECES // 2)
+        plain_last = range(PIECES // 2, PIECES)
+
+        def project_x_dst(c, opens):
+            for side in range(SIDES):
+                nc.tensor.matmul(
+                    maps[c][side][:],
+                    w_dst_side[:, side, :],
+                    x_dst_sb[:, c * PIECE : (c + 1) * PIECE],
+                    start=opens,
+                    stop=not opens,
+                )
+
+        for c in plain_first:
+            project_x_dst(c, opens=True)
         for c in range(PIECES):
             looked_up = table_sb[:].indirect(offsets[:, c * (PIECE // 16) : (c + 1) * (PIECE // 16)])
             for side in range(SIDES):
-                nc.tensor.matmul(maps[c][side][:], w_src_side[:, side, :], looked_up, start=True, stop=False)
-        for c in range(PIECES):
-            for side in range(SIDES):
                 nc.tensor.matmul(
-                    maps[c][side][:], w_dst_side[:, side, :], x_dst_sb[:, c * PIECE : (c + 1) * PIECE], start=False, stop=True
+                    maps[c][side][:], w_src_side[:, side, :], looked_up, start=(c in plain_last), stop=(c in plain_first)
                 )
+        for c in plain_last:
+            project_x_dst(c, opens=False)
 
         e = [held.tile([P, SIDES, PIECE], F32, name=f"e{c}") for c in range(PIECES)]
         e_bf = [held.tile([P, SIDES, PIECE], BF16, name=f"e_bf{c}") for c in range(PIECES)]

@@ -30,21 +30,21 @@ def tile_attentionsheaflearner_kernel(tc, table, x_dst, w_src, w_dst, grp, diag,
         tc.tile_pool(name="held", bufs=1) as held,
         tc.psum_pool(name="psum", bufs=PSUM_BANKS) as psum,
     ):
-        x_dst_sb = held.tile([P, N], BF16, name="x_dst_sb")
-        nc.sync.dma_start(x_dst_sb[:, 0 : N // 2], x_dst[:, 0 : N // 2])
-        w_dst_sb = held.tile([P, M], BF16, name="w_dst_sb")
-        nc.scalar.dma_start(w_dst_sb[:], w_dst)
         offsets = held.tile([P, N // 16], U16, name="offsets")
         nc.sync.dma_start(offsets[:], offs)
         w_src_sb = held.tile([P, M], BF16, name="w_src_sb")
         nc.scalar.dma_start(w_src_sb[:], w_src)
         table_sb = held.tile([P, S], BF16, name="table_sb")
         nc.sync.dma_start(table_sb[:], table)
-        nc.sync.dma_start(x_dst_sb[:, N // 2 : N], x_dst[:, N // 2 : N])
+        w_dst_sb = held.tile([P, M], BF16, name="w_dst_sb")
+        nc.scalar.dma_start(w_dst_sb[:], w_dst)
+        x_dst_sb = held.tile([P, N], BF16, name="x_dst_sb")
+        nc.sync.dma_start(x_dst_sb[:], x_dst)
 
         w_src_side = held.tile([P, SIDES, P], BF16, name="w_src_side")
         nc.vector.tensor_copy(w_src_side[:], w_src_sb[:].rearrange("d (p side) -> d side p", side=SIDES))
-        w_dst_side = w_dst_sb[:].rearrange("d (p side) -> d side p", side=SIDES)
+        w_dst_side = held.tile([P, SIDES, P], BF16, name="w_dst_side")
+        nc.vector.tensor_copy(w_dst_side[:], w_dst_sb[:].rearrange("d (p side) -> d side p", side=SIDES))
         out_side = out.rearrange("(p side) j -> side p j", side=SIDES)
         diag_sb = held.tile([P, SIDES], F32, name="diag_sb")
         nc.scalar.dma_start(diag_sb[:], diag.rearrange("(p side) one -> p (side one)", side=SIDES))
@@ -63,29 +63,15 @@ def tile_attentionsheaflearner_kernel(tc, table, x_dst, w_src, w_dst, grp, diag,
         make_identity(nc, ident[:])
 
         maps = [[psum.tile([P, PIECE], F32, name=f"maps{c}{side}", tag="bank") for side in range(SIDES)] for c in range(PIECES)]
-        plain_first = range(PIECES // 2)
-        plain_last = range(PIECES // 2, PIECES)
-
-        def project_x_dst(c, opens):
-            for side in range(SIDES):
-                nc.tensor.matmul(
-                    maps[c][side][:],
-                    w_dst_side[:, side, :],
-                    x_dst_sb[:, c * PIECE : (c + 1) * PIECE],
-                    start=opens,
-                    stop=not opens,
-                )
-
-        for c in plain_first:
-            project_x_dst(c, opens=True)
         for c in range(PIECES):
             looked_up = table_sb[:].indirect(offsets[:, c * (PIECE // 16) : (c + 1) * (PIECE // 16)])
             for side in range(SIDES):
+                nc.tensor.matmul(maps[c][side][:], w_src_side[:, side, :], looked_up, start=True, stop=False)
+        for c in range(PIECES):
+            for side in range(SIDES):
                 nc.tensor.matmul(
-                    maps[c][side][:], w_src_side[:, side, :], looked_up, start=(c in plain_last), stop=(c in plain_first)
+                    maps[c][side][:], w_dst_side[:, side, :], x_dst_sb[:, c * PIECE : (c + 1) * PIECE], start=False, stop=True
                 )
-        for c in plain_last:
-            project_x_dst(c, opens=False)
 
         e = [held.tile([P, SIDES, PIECE], F32, name=f"e{c}") for c in range(PIECES)]
         e_bf = [held.tile([P, SIDES, PIECE], BF16, name=f"e_bf{c}") for c in range(PIECES)]
@@ -119,14 +105,13 @@ def tile_attentionsheaflearner_kernel(tc, table, x_dst, w_src, w_dst, grp, diag,
             rden_all = psum.tile([P, PIECE], F32, name="rden_all", tag="bank")
             for i in range(BLOCKS):
                 nc.tensor.transpose(rden_all[:, i * P : (i + 1) * P], rden_wide[c][:, i * P : (i + 1) * P], ident[:])
-            share = held.tile([P, SIDES, PIECE], F32, name=f"share{c}")
-            nc.vector.tensor_tensor(
-                share[:], e[c][:], rden_all[:].unsqueeze(1).to_broadcast([P, SIDES, PIECE]), MULT
-            )
+            share = [held.tile([P, PIECE], F32, name=f"share{c}{side}") for side in range(SIDES)]
             res = [held.tile([P, PIECE], F32, name=f"res{c}{side}") for side in range(SIDES)]
-            nc.scalar.activation(res[0][:], share[:, 0, :], IDENTITY, bias=diag_sb[:, 0:1], scale=-1.0)
-            nc.gpsimd.tensor_scalar(res[1][:], share[:, 1, :], -1.0, diag_sb[:, 1:2], MULT, ADD)
-            for side in range(SIDES):
+            nc.vector.tensor_tensor(share[1][:], e[c][:, 1, :], rden_all[:], MULT)
+            nc.gpsimd.tensor_scalar(res[1][:], share[1][:], -1.0, diag_sb[:, 1:2], MULT, ADD)
+            nc.vector.tensor_tensor(share[0][:], e[c][:, 0, :], rden_all[:], MULT)
+            nc.scalar.activation(res[0][:], share[0][:], IDENTITY, bias=diag_sb[:, 0:1], scale=-1.0)
+            for side in reversed(range(SIDES)):
                 nc.sync.dma_start(out_side[side, :, c * PIECE : (c + 1) * PIECE], res[side][:])
 
         for c in range(PIECES):

@@ -78,10 +78,17 @@ def tile_attentionsheaflearner_kernel(tc, table, x_dst, w_src, w_dst, grp, diag,
         rden_t = [held.tile([P, BLOCKS * GROUPS], F32, name=f"rden_t{c}") for c in range(PIECES)]
         rden_wide = [held.tile([P, BLOCKS * P], F32, name=f"rden_wide{c}") for c in range(PIECES)]
 
+        def numerator(c, side):
+            nc.scalar.activation(e[c][:, side, :], maps[c][side][:], EXP)
+
         def exponentials(c):
             for side in range(SIDES):
-                nc.scalar.activation(e[c][:, side, :], maps[c][side][:], EXP)
+                numerator(c, side)
                 nc.vector.tensor_copy(e_bf[c][:, side, :], e[c][:, side, :])
+
+        def rounded_exponentials(c):
+            for side in range(SIDES):
+                nc.scalar.activation(e_bf[c][:, side, :], maps[c][side][:], EXP)
 
         def reciprocals(c):
             den_t = psum.tile([P, BLOCKS * GROUPS], F32, name="den_t", tag="bank")
@@ -114,9 +121,14 @@ def tile_attentionsheaflearner_kernel(tc, table, x_dst, w_src, w_dst, grp, diag,
             for side in reversed(range(SIDES)):
                 nc.sync.dma_start(out_side[side, :, c * PIECE : (c + 1) * PIECE], res[side][:])
 
-        for c in range(PIECES):
+        last = PIECES - 1
+        for c in range(last):
             exponentials(c)
-        for c in range(PIECES):
+        rounded_exponentials(last)
+        for c in range(last):
             reciprocals(c)
+            if c < SIDES:
+                numerator(last, c)
+        reciprocals(last)
         for c in range(PIECES):
             results(c)

@@ -102,11 +102,12 @@ def tile_attentionsheaflearner_kernel(tc, table, x_dst, w_src, w_dst, grp, diag,
                         stop=(side == SIDES - 1),
                     )
             nc.vector.reciprocal(rden_t[c][:], den_t[:])
-            nc.scalar.activation(
-                rden_wide[c][:].rearrange("j (g q) -> j g q", q=REPLICAS),
-                rden_t[c][:].unsqueeze(2).to_broadcast([P, BLOCKS * GROUPS, REPLICAS]),
-                COPY,
-            )
+            wide = rden_wide[c][:].rearrange("j (g q) -> j g q", q=REPLICAS)
+            narrow = rden_t[c][:].unsqueeze(2).to_broadcast([P, BLOCKS * GROUPS, REPLICAS])
+            if c < PIECES // 2:
+                nc.vector.tensor_copy(wide, narrow)
+            else:
+                nc.scalar.activation(wide, narrow, COPY)
 
         def results(c):
             rden_all = psum.tile([P, PIECE], F32, name="rden_all", tag="bank")

@@ -122,14 +122,15 @@ def tile_attentionsheaflearner_kernel(tc, table, x_dst, w_src, w_dst, grp, diag,
             for side in reversed(range(SIDES)):
                 nc.sync.dma_start(out_side[side, :, c * PIECE : (c + 1) * PIECE], res[side][:])
 
-        last = PIECES - 1
-        for c in range(last):
+        half = PIECES // 2
+        for c in range(half):
             exponentials(c)
-        rounded_exponentials(last)
-        for c in range(last):
+        for c in range(half, PIECES):
+            rounded_exponentials(c)
+        for c in range(PIECES):
             reciprocals(c)
-            if c < SIDES:
-                numerator(last, c)
-        reciprocals(last)
+            if c < half:
+                for side in range(SIDES):
+                    numerator(half + c, side)
         for c in range(PIECES):
             results(c)

@@ -30,12 +30,12 @@ def tile_attentionsheaflearner_kernel(tc, table, x_dst, w_src, w_dst, grp, diag,
         tc.tile_pool(name="held", bufs=1) as held,
         tc.psum_pool(name="psum", bufs=PSUM_BANKS) as psum,
     ):
+        w_src_sb = held.tile([P, M], BF16, name="w_src_sb")
+        nc.sync.dma_start(w_src_sb[:], w_src)
+        table_sb = held.tile([P, S], BF16, name="table_sb")
+        nc.scalar.dma_start(table_sb[:], table)
         offsets = held.tile([P, N // 16], U16, name="offsets")
         nc.sync.dma_start(offsets[:], offs)
-        w_src_sb = held.tile([P, M], BF16, name="w_src_sb")
-        nc.scalar.dma_start(w_src_sb[:], w_src)
-        table_sb = held.tile([P, S], BF16, name="table_sb")
-        nc.sync.dma_start(table_sb[:], table)
         w_dst_sb = held.tile([P, M], BF16, name="w_dst_sb")
         nc.scalar.dma_start(w_dst_sb[:], w_dst)
         x_dst_sb = held.tile([P, N], BF16, name="x_dst_sb")

import concourse.mybir as mybir
from concourse.masks import make_identity

BF16, F32, U16 = mybir.dt.bfloat16, mybir.dt.float32, mybir.dt.uint16
EXP, COPY, IDENTITY = (
    mybir.ActivationFunctionType.Exp,
    mybir.ActivationFunctionType.Copy,
    mybir.ActivationFunctionType.Identity,
)
MULT, ADD = mybir.AluOpType.mult, mybir.AluOpType.add

P = 128
S = 256
N = 1024
M = 256
SIDES = M // P
PIECE = 256
PIECES = N // PIECE
PSUM_BANKS = 8
REPLICAS = 16 // SIDES
GROUPS = P // REPLICAS
BLOCKS = PIECE // P

FLOPS = 2 * (2 * P) * M * N + 2 * P * M * N


def tile_attentionsheaflearner_kernel(tc, table, x_dst, w_src, w_dst, grp, diag, offs, out):
    nc = tc.nc
    with (
        tc.tile_pool(name="held", bufs=1) as held,
        tc.psum_pool(name="psum", bufs=PSUM_BANKS) as psum,
    ):
        w_src_sb = held.tile([P, M], BF16, name="w_src_sb")
        nc.sync.dma_start(w_src_sb[:], w_src)
        table_sb = held.tile([P, S], BF16, name="table_sb")
        nc.scalar.dma_start(table_sb[:], table)
        offsets = held.tile([P, N // 16], U16, name="offsets")
        nc.sync.dma_start(offsets[:], offs)
        w_dst_sb = held.tile([P, M], BF16, name="w_dst_sb")
        nc.scalar.dma_start(w_dst_sb[:], w_dst)
        x_dst_sb = held.tile([P, N], BF16, name="x_dst_sb")
        nc.sync.dma_start(x_dst_sb[:], x_dst)

        w_src_side = held.tile([P, SIDES, P], BF16, name="w_src_side")
        nc.vector.tensor_copy(w_src_side[:], w_src_sb[:].rearrange("d (p side) -> d side p", side=SIDES))
        w_dst_side = held.tile([P, SIDES, P], BF16, name="w_dst_side")
        nc.vector.tensor_copy(w_dst_side[:], w_dst_sb[:].rearrange("d (p side) -> d side p", side=SIDES))
        out_side = out.rearrange("(p side) j -> side p j", side=SIDES)
        diag_sb = held.tile([P, SIDES], F32, name="diag_sb")
        nc.scalar.dma_start(diag_sb[:], diag.rearrange("(p side) one -> p (side one)", side=SIDES))

        grp_rows = held.tile([P, P], BF16, name="grp_rows")
        group_of = held.tile([P, GROUPS], BF16, name="group_of")
        nc.vector.memset(group_of[:], 0.0)
        for half in range(2):
            rows = slice(half * (P // 2), (half + 1) * (P // 2))
            nc.scalar.dma_start(grp_rows[rows, :], grp.rearrange("(q two) r -> two q r", two=2)[0])
            nc.vector.tensor_copy(
                group_of[rows, half * (GROUPS // 2) : (half + 1) * (GROUPS // 2)],
                grp_rows[:].rearrange("q (a b) -> q b a", b=16)[rows, 0, :],
            )
        ident = held.tile([P, P], F32, name="ident")
        make_identity(nc, ident[:])

        maps = [[psum.tile([P, PIECE], F32, name=f"maps{c}{side}", tag="bank") for side in range(SIDES)] for c in range(PIECES)]
        for c in range(PIECES):
            looked_up = table_sb[:].indirect(offsets[:, c * (PIECE // 16) : (c + 1) * (PIECE // 16)])
            for side in range(SIDES):
                nc.tensor.matmul(maps[c][side][:], w_src_side[:, side, :], looked_up, start=True, stop=False)
        for c in range(PIECES):
            for side in range(SIDES):
                nc.tensor.matmul(
                    maps[c][side][:], w_dst_side[:, side, :], x_dst_sb[:, c * PIECE : (c + 1) * PIECE], start=False, stop=True
                )

        e = [held.tile([P, SIDES, PIECE], F32, name=f"e{c}") for c in range(PIECES)]
        e_bf = [held.tile([P, SIDES, PIECE], BF16, name=f"e_bf{c}") for c in range(PIECES)]
        rden_t = [held.tile([P, BLOCKS * GROUPS], F32, name=f"rden_t{c}") for c in range(PIECES)]
        rden_wide = [held.tile([P, BLOCKS * P], F32, name=f"rden_wide{c}") for c in range(PIECES)]

        def numerator(c, side):
            nc.scalar.activation(e[c][:, side, :], maps[c][side][:], EXP)

        def exponentials(c):
            for side in range(SIDES):
                numerator(c, side)
                nc.vector.tensor_copy(e_bf[c][:, side, :], e[c][:, side, :])

        def rounded_exponentials(c):
            for side in range(SIDES):
                nc.scalar.activation(e_bf[c][:, side, :], maps[c][side][:], EXP)

        def reciprocals(c):
            den_t = psum.tile([P, BLOCKS * GROUPS], F32, name="den_t", tag="bank")
            for i in range(BLOCKS):
                for side in range(SIDES):
                    nc.tensor.matmul(
                        den_t[:, i * GROUPS : (i + 1) * GROUPS],
                        e_bf[c][:, side, i * P : (i + 1) * P],
                        group_of[:],
                        start=(side == 0),
                        stop=(side == SIDES - 1),
                    )
            nc.vector.reciprocal(rden_t[c][:], den_t[:])
            wide = rden_wide[c][:].rearrange("j (g q) -> j g q", q=REPLICAS)
            narrow = rden_t[c][:].unsqueeze(2).to_broadcast([P, BLOCKS * GROUPS, REPLICAS])
            if c < PIECES // 2:
                nc.vector.tensor_copy(wide, narrow)
            else:
                nc.scalar.activation(wide, narrow, COPY)

        def results(c):
            rden_all = psum.tile([P, PIECE], F32, name="rden_all", tag="bank")
            for i in range(BLOCKS):
                nc.tensor.transpose(rden_all[:, i * P : (i + 1) * P], rden_wide[c][:, i * P : (i + 1) * P], ident[:])
            share = [held.tile([P, PIECE], F32, name=f"share{c}{side}") for side in range(SIDES)]
            res = [held.tile([P, PIECE], F32, name=f"res{c}{side}") for side in range(SIDES)]
            nc.vector.tensor_tensor(share[1][:], e[c][:, 1, :], rden_all[:], MULT)
            nc.gpsimd.tensor_scalar(res[1][:], share[1][:], -1.0, diag_sb[:, 1:2], MULT, ADD)
            nc.vector.tensor_tensor(share[0][:], e[c][:, 0, :], rden_all[:], MULT)
            nc.scalar.activation(res[0][:], share[0][:], IDENTITY, bias=diag_sb[:, 0:1], scale=-1.0)
            for side in reversed(range(SIDES)):
                nc.sync.dma_start(out_side[side, :, c * PIECE : (c + 1) * PIECE], res[side][:])

        half = PIECES // 2
        for c in range(half):
            exponentials(c)
        for c in range(half, PIECES):
            rounded_exponentials(c)
        for c in range(PIECES):
            reciprocals(c)
            if c < half:
                for side in range(SIDES):
                    numerator(half + c, side)
        for c in range(PIECES):
            results(c)
